import numpy as np
import ml_dtypes


def mxq(x, axis, fmt="e4m3"):
    dtype, down = {"e4m3": (ml_dtypes.float8_e4m3fn, 7), "e5m2": (ml_dtypes.float8_e5m2, 14)}[fmt]
    v = np.moveaxis(np.asarray(x, np.float32).astype(ml_dtypes.bfloat16).astype(np.float64), axis, -1)
    blocks = v.reshape(v.shape[:-1] + (-1, 32))
    amax = np.abs(blocks).max(-1, keepdims=True)
    byte = np.maximum(np.where(amax > 0, np.frexp(amax)[1] - 1 + 127, 0) - down, 1)
    scale = np.exp2(byte - 127.0)
    codes = (blocks / scale).astype(np.float32).astype(dtype).astype(np.float64)
    return np.moveaxis((codes * scale).reshape(v.shape), -1, axis)


WIDE = False


def mx_kscale(k):
    if not WIDE:
        return np.ones(k)
    levels = np.array([10, -10, 5, -5, 0])
    if k % 512:
        return np.exp2(np.random.permutation(np.resize(levels, k // 32))).repeat(32)
    a = np.empty((k // 512, 16))
    for p in range(k // 512):
        a[p, :8] = np.random.permutation(np.resize(levels, 8))
        for g in range(8):
            far = levels[np.abs(levels - a[p, g]) >= 10]
            a[p, g + 8] = far[np.random.randint(len(far))]
    return np.exp2(a.ravel()).repeat(32)


BF16 = ml_dtypes.bfloat16


def bf(x):
    return np.asarray(x, np.float32).astype(BF16)


def f64(x):
    return np.asarray(x).astype(np.float64)


B, I, H, P = 8192, 256, 256, 2048
C = I + H


def sigmoid(v):
    return 1.0 / (1.0 + np.exp(-v))


def setup_inputs():
    s = mx_kscale(C)
    return {"x": bf(np.random.standard_normal((B, I)) * s[:I]),
            "rh": bf(np.random.standard_normal((B, H)) * 0.95 * s[I:]),
            "update": bf(np.random.standard_normal((B, H)) * 0.7),
            "hidden": bf(1.5 + np.random.standard_normal((B, H))),
            "Wn": bf(np.random.standard_normal((H, C)) / np.sqrt(C) / s[None, :]),
            "bn": bf(-0.1 + 0.2 * np.random.standard_normal(H)),
            "connection_strength": bf(1.0 + 0.3 * np.random.standard_normal(H)),
            "connection_decay": bf(0.4 + 0.2 * np.random.random(1)),
            "connection_history": bf(2.0 * np.random.standard_normal(H))}


def reference(x, rh, update, hidden, Wn, bn, connection_strength, connection_decay, connection_history):
    h = f64(hidden)
    u = f64(update)
    activity = np.mean(np.abs(h), axis=0)
    ch = f64(connection_history) * f64(connection_decay) + activity
    cs = f64(connection_strength) * sigmoid(ch)
    combined_reset = np.concatenate([f64(x), f64(rh)], axis=1)
    new = (mxq(combined_reset, 1, "e4m3") @ mxq(f64(Wn), 1, "e4m3").T) + f64(bn)
    return (1.0 - u) * h + u * new * cs[None, :]

@@ -1,0 +1,280 @@
+from contextlib import ExitStack
+
+import concourse.mybir as mybir
+from concourse.masks import make_identity
+
+F32 = mybir.dt.float32
+BF16 = mybir.dt.bfloat16
+U32 = mybir.dt.uint32
+U8 = mybir.dt.uint8
+FP8X4 = mybir.dt.float8_e4m3fn_x4
+ALU = mybir.AluOpType
+ACT = mybir.ActivationFunctionType
+
+P = 128
+B = 8192
+H = 256
+HALVES = H // P
+ROW_TILES = B // P
+GROUP_TILES = 4
+GROUP_ROWS = GROUP_TILES * P
+GROUP_COLS = GROUP_TILES * H
+CHUNK_GROUPS = 2
+CHUNK_COLS = CHUNK_GROUPS * GROUP_COLS
+CHUNKS = ROW_TILES // (GROUP_TILES * CHUNK_GROUPS)
+BANK_TILES = 2
+GROUPS = ROW_TILES // GROUP_TILES
+LOAD_BUFS = 4
+ONES_COLS = 2
+GPSIMD_TILES = 2
+MATMUL_EVERY = 3
+
+FLOPS = 2 * B * (2 * H) * H
+
+
+def tile_persistentgrucell_pb_t_kernel(
+    tc,
+    x,
+    rh,
+    update,
+    hidden,
+    Wn,
+    bn,
+    connection_strength,
+    connection_decay,
+    connection_history,
+    out,
+):
+    nc = tc.nc
+    x_rows = x.rearrange("(p t) k -> p (t k)", t=ROW_TILES)
+    rh_rows = rh.rearrange("(p t) k -> p (t k)", t=ROW_TILES)
+    u_rows = update.rearrange("(p t) k -> p (t k)", t=ROW_TILES)
+    h_rows = hidden.rearrange("(p t) k -> p (t k)", t=ROW_TILES)
+    out_rows = out.rearrange("(p t) k -> p (t k)", t=ROW_TILES)
+
+    with ExitStack() as ctx:
+        const = ctx.enter_context(tc.tile_pool(name="const", bufs=1))
+        keep = ctx.enter_context(tc.tile_pool(name="keep", bufs=1))
+        loads = ctx.enter_context(tc.tile_pool(name="loads", bufs=LOAD_BUFS))
+        work = ctx.enter_context(tc.tile_pool(name="work", bufs=3))
+        psum = ctx.enter_context(tc.psum_pool(name="psum", bufs=2))
+        ctx.enter_context(tc.manual_schedule())
+
+        vec_rows = const.tile([P, P], BF16)
+        nc.vector.memset(vec_rows[:], 0.0)
+        for r, vec in enumerate((bn, connection_strength, connection_history)):
+            nc.scalar.dma_start(
+                out=vec_rows[HALVES * r : HALVES * (r + 1), :],
+                in_=vec.rearrange("(a c) -> a c", a=HALVES),
+            )
+        decay_bf16 = const.tile([P, 1], BF16)
+        nc.scalar.dma_start(out=decay_bf16[:], in_=connection_decay.partition_broadcast(P))
+        w_sb = const.tile([P, HALVES * 2 * H], BF16)
+        nc.sync.dma_start(
+            out=w_sb[:].rearrange("p (a k) -> p a k", a=HALVES),
+            in_=Wn.rearrange("(a p) k -> p a k", p=P),
+        )
+        table_warm = const.tile([P, 1], F32)
+        nc.vector.memset(table_warm[:], 0.0)
+        nc.scalar.activation(out=table_warm[:], in_=table_warm[:], func=ACT.Tanh)
+        ident_f32 = const.tile([P, P], F32)
+        make_identity(nc, ident_f32[:])
+        ident_bf16 = const.tile([P, P], BF16)
+        make_identity(nc, ident_bf16[:])
+        ones = const.tile([P, ONES_COLS], BF16)
+        nc.vector.memset(ones[:], 1.0)
+
+        w_words = w_sb[:].bitcast(F32)
+        wt_ps = psum.tile([P, 2, H], F32, tag="xt_ps")
+        for a in range(HALVES):
+            for s in range(2):
+                nc.tensor.transpose(
+                    wt_ps[:, s, a * P : (a + 1) * P],
+                    w_words[:, a * 2 * P + s : (a + 1) * 2 * P : 2],
+                    ident_f32[:],
+                )
+        w_grouped = const.tile([P, 4 * H], BF16, align_bytes=64)
+        nc.vector.tensor_copy(
+            out=w_grouped[:].bitcast(F32).rearrange("q (n s) -> q n s", s=2),
+            in_=wt_ps[:].rearrange("q s n -> q n s"),
+        )
+        w_codes = const.tile([P, H], U32, align_bytes=64)
+        w_scales = const.tile([P, H], U8, align_bytes=64)
+        nc.vector.quantize_mx(out=w_codes[:].bitcast(FP8X4), scales=w_scales[:], in_=w_grouped[:])
+
+        vec_ps = psum.tile([P, P], BF16, tag="acc_ps")
+        nc.tensor.transpose(vec_ps[:], vec_rows[:], ident_bf16[:])
+        vec_cols = const.tile([P, 3 * HALVES], F32)
+        nc.vector.tensor_copy(out=vec_cols[:], in_=vec_ps[:, 0 : 3 * HALVES])
+        bn_col = vec_cols[:, 0:HALVES]
+        strength_col = vec_cols[:, HALVES : 2 * HALVES]
+        history_col = vec_cols[:, 2 * HALVES : 3 * HALVES]
+        decay_col = const.tile([P, 1], F32)
+        nc.vector.tensor_copy(out=decay_col[:], in_=decay_bf16[:])
+        half_decayed = const.tile([P, HALVES], F32)
+        nc.vector.tensor_scalar(
+            out=half_decayed[:], in0=history_col, scalar1=decay_col[:, 0:1], scalar2=0.5, op0=ALU.mult, op1=ALU.mult
+        )
+        half_strength = const.tile([P, HALVES], F32)
+        nc.vector.tensor_scalar(out=half_strength[:], in0=strength_col, scalar1=0.5, scalar2=None, op0=ALU.mult)
+
+        act_ps = [psum.tile([P, ONES_COLS], F32, tag="s_ps", bufs=4, name="act_ps%d" % a) for a in range(HALVES)]
+        u_sb = []
+        blend_sb = []
+        for c in range(CHUNKS):
+            chunk_cols = slice(c * CHUNK_COLS, (c + 1) * CHUNK_COLS)
+            h_chunk = keep.tile([P, CHUNK_COLS], BF16, name="h_chunk%d" % c)
+            nc.sync.dma_start(out=h_chunk[:], in_=h_rows[:, chunk_cols])
+            u_chunk = keep.tile([P, CHUNK_COLS], BF16, name="u_chunk%d" % c)
+            u_sb.append(u_chunk)
+            nc.sync.dma_start(out=u_chunk[:], in_=u_rows[:, chunk_cols])
+            h_abs = work.tile([P, CHUNK_COLS], BF16)
+            nc.scalar.activation(out=h_abs[:], in_=h_chunk[:], func=ACT.Abs)
+            blocks = CHUNK_COLS // P
+            for k in range(blocks):
+                nc.tensor.matmul(
+                    out=act_ps[k % HALVES][:],
+                    lhsT=h_abs[:, k * P : (k + 1) * P],
+                    rhs=ones[:],
+                    start=(c == 0 and k < HALVES),
+                    stop=(c == CHUNKS - 1 and k >= blocks - HALVES),
+                )
+            blend_chunk = keep.tile([P, CHUNK_COLS], F32, name="blend_chunk%d" % c)
+            blend_sb.append(blend_chunk)
+            nc.vector.scalar_tensor_tensor(
+                out=blend_chunk[:],
+                in0=u_chunk[:],
+                scalar=1.0,
+                in1=h_chunk[:],
+                op0=ALU.subtract,
+                op1=ALU.mult,
+            )
+
+        tanh_col = const.tile([P, HALVES], F32)
+        for a in range(HALVES):
+            nc.scalar.activation(
+                out=tanh_col[:, a : a + 1],
+                in_=act_ps[a][:, 0:1],
+                func=ACT.Tanh,
+                bias=half_decayed[:, a : a + 1],
+                scale=0.5 / B,
+            )
+        cs_col = const.tile([P, HALVES], F32)
+        nc.vector.scalar_tensor_tensor(
+            out=cs_col[:], in0=tanh_col[:], scalar=1.0, in1=half_strength[:], op0=ALU.add, op1=ALU.mult
+        )
+        bias_col = const.tile([P, HALVES], F32)
+        nc.vector.tensor_tensor(out=bias_col[:], in0=bn_col, in1=cs_col[:], op=ALU.mult)
+
+        xr_words = {}
+        grouped_of = {}
+        codes_of = {}
+        scales_of = {}
+        scaled_of = {}
+        gated_of = {}
+
+        def load_inputs(c):
+            chunk_cols = slice(c * CHUNK_COLS, (c + 1) * CHUNK_COLS)
+            xr_chunk = loads.tile([P, 2 * CHUNK_COLS], BF16)
+            xr_view = xr_chunk[:].rearrange("p (t j k) -> p t j k", j=2, k=H)
+            nc.sync.dma_start(out=xr_view[:, :, 0, :], in_=x_rows[:, chunk_cols].rearrange("p (t k) -> p t k", k=H))
+            nc.sync.dma_start(out=xr_view[:, :, 1, :], in_=rh_rows[:, chunk_cols].rearrange("p (t k) -> p t k", k=H))
+            xr_words[c] = xr_chunk[:].bitcast(F32)
+
+        def transpose_inputs(g, j):
+            c, gi = divmod(g, CHUNK_GROUPS)
+            if j == 0:
+                grouped = work.tile([P, 4 * GROUP_ROWS], BF16, align_bytes=64)
+                grouped_of[g] = grouped
+            grouped_words = grouped_of[g][:].bitcast(F32).rearrange("q (n s) -> q n s", s=2)
+            xt_ps = psum.tile([P, 2, BANK_TILES * P], F32)
+            for i in range(BANK_TILES):
+                t = gi * GROUP_TILES + j * BANK_TILES + i
+                for s in range(2):
+                    nc.tensor.transpose(
+                        xt_ps[:, s, i * P : (i + 1) * P],
+                        xr_words[c][:, t * 2 * P + s : (t + 1) * 2 * P : 2],
+                        ident_f32[:],
+                    )
+            nc.scalar.copy(
+                out=grouped_words[:, j * BANK_TILES * P : (j + 1) * BANK_TILES * P, :],
+                in_=xt_ps[:].rearrange("q s n -> q n s"),
+            )
+
+        def quantise(g):
+            codes = work.tile([P, GROUP_ROWS], U32, align_bytes=64)
+            scales = work.tile([P, GROUP_ROWS], U8, align_bytes=64)
+            nc.vector.quantize_mx(out=codes[:].bitcast(FP8X4), scales=scales[:], in_=grouped_of[g][:])
+            codes_of[g] = codes
+            scales_of[g] = scales
+
+        def multiply(g):
+            scaled = work.tile([P, HALVES, GROUP_ROWS], F32)
+            for a in range(HALVES):
+                acc_ps = psum.tile([P, GROUP_ROWS], F32)
+                nc.tensor.matmul_mx(
+                    out=acc_ps[:],
+                    lhsT=w_codes[:, a * P : (a + 1) * P].bitcast(FP8X4),
+                    lhsT_scale=w_scales[:, a * P : (a + 1) * P],
+                    rhs=codes_of[g][:].bitcast(FP8X4),
+                    rhs_scale=scales_of[g][:],
+                    start=True,
+                    stop=True,
+                )
+                nc.scalar.activation(
+                    out=scaled[:, a, :],
+                    in_=acc_ps[:],
+                    func=ACT.Identity,
+                    bias=bias_col[:, a : a + 1],
+                    scale=cs_col[:, a : a + 1],
+                )
+            scaled_of[g] = scaled
+
+        def gate_rows(g, j):
+            c, gi = divmod(g, CHUNK_GROUPS)
+            if j == 0:
+                gated = work.tile([P, GROUP_COLS], F32)
+                gated_of[g] = gated
+            s_ps = psum.tile([P, BANK_TILES * H], F32, bufs=4)
+            for i in range(BANK_TILES):
+                n0 = (j * BANK_TILES + i) * P
+                for a in range(HALVES):
+                    block = s_ps[:, i * H + a * P : i * H + (a + 1) * P]
+                    if ((j * BANK_TILES + i) * HALVES + a) % MATMUL_EVERY == 0:
+                        nc.tensor.matmul(
+                            out=block, lhsT=scaled_of[g][:, a, n0 : n0 + P], rhs=ident_f32[:], start=True, stop=True
+                        )
+                    else:
+                        nc.tensor.transpose(block, scaled_of[g][:, a, n0 : n0 + P], ident_f32[:])
+            bank = slice(j * BANK_TILES * H, (j + 1) * BANK_TILES * H)
+            u_bank = slice(gi * GROUP_COLS + j * BANK_TILES * H, gi * GROUP_COLS + (j + 1) * BANK_TILES * H)
+            nc.vector.tensor_tensor(out=gated_of[g][:, bank], in0=s_ps[:], in1=u_sb[c][:, u_bank], op=ALU.mult)
+
+        def finish_rows(g):
+            c, gi = divmod(g, CHUNK_GROUPS)
+            group_cols = slice(gi * GROUP_COLS, (gi + 1) * GROUP_COLS)
+            split = GROUP_COLS - GPSIMD_TILES * H
+            for engine, lo, hi in ((nc.vector, 0, split), (nc.gpsimd, split, GROUP_COLS)):
+                cols = slice(gi * GROUP_COLS + lo, gi * GROUP_COLS + hi)
+                engine.tensor_tensor(
+                    out=blend_sb[c][:, cols], in0=gated_of[g][:, lo:hi], in1=blend_sb[c][:, cols], op=ALU.subtract
+                )
+            nc.sync.dma_start(out=out_rows[:, g * GROUP_COLS : (g + 1) * GROUP_COLS], in_=blend_sb[c][:, group_cols])
+
+        for c in range(LOAD_BUFS):
+            load_inputs(c)
+        for i in range(-3, GROUPS):
+            if 0 <= i + 1 < GROUPS:
+                multiply(i + 1)
+            if 0 <= i + 2 < GROUPS:
+                quantise(i + 2)
+            for j in range(GROUP_TILES // BANK_TILES):
+                if 0 <= i:
+                    gate_rows(i, j)
+                if i + 3 < GROUPS:
+                    transpose_inputs(i + 3, j)
+            if 0 <= i:
+                finish_rows(i)
+            c, gi = divmod(i + 3, CHUNK_GROUPS)
+            if gi == CHUNK_GROUPS - 1 and c + LOAD_BUFS < CHUNKS:
+                load_inputs(c + LOAD_BUFS)

@@ -5,6 +5,7 @@ from concourse.masks import make_identity
 
 F32 = mybir.dt.float32
 BF16 = mybir.dt.bfloat16
+I32 = mybir.dt.int32
 U32 = mybir.dt.uint32
 U8 = mybir.dt.uint8
 FP8X4 = mybir.dt.float8_e4m3fn_x4
@@ -16,18 +17,21 @@ B = 8192
 H = 256
 HALVES = H // P
 ROW_TILES = B // P
+BANK_TILES = 2
+BANK_COLS = BANK_TILES * H
 GROUP_TILES = 4
+GROUP_BANKS = GROUP_TILES // BANK_TILES
 GROUP_ROWS = GROUP_TILES * P
 GROUP_COLS = GROUP_TILES * H
-CHUNK_GROUPS = 2
-CHUNK_COLS = CHUNK_GROUPS * GROUP_COLS
-CHUNKS = ROW_TILES // (GROUP_TILES * CHUNK_GROUPS)
-BANK_TILES = 2
 GROUPS = ROW_TILES // GROUP_TILES
-LOAD_BUFS = 4
+CHUNK_GROUPS = 2
+CHUNK_TILES = CHUNK_GROUPS * GROUP_TILES
+CHUNK_COLS = CHUNK_GROUPS * GROUP_COLS
+CHUNKS = GROUPS // CHUNK_GROUPS
+EARLY_CHUNKS = 2
+EARLY_GROUPS = EARLY_CHUNKS * CHUNK_GROUPS
 ONES_COLS = 2
-GPSIMD_TILES = 2
-MATMUL_EVERY = 3
+SIGN_OFF = 0x7FFF7FFF
 
 FLOPS = 2 * B * (2 * H) * H
 
@@ -46,8 +50,8 @@ def tile_persistentgrucell_pb_t_kernel(
     out,
 ):
     nc = tc.nc
-    x_rows = x.rearrange("(p t) k -> p (t k)", t=ROW_TILES)
-    rh_rows = rh.rearrange("(p t) k -> p (t k)", t=ROW_TILES)
+    x_rows = x.rearrange("(p t) k -> p t k", t=ROW_TILES)
+    rh_rows = rh.rearrange("(p t) k -> p t k", t=ROW_TILES)
     u_rows = update.rearrange("(p t) k -> p (t k)", t=ROW_TILES)
     h_rows = hidden.rearrange("(p t) k -> p (t k)", t=ROW_TILES)
     out_rows = out.rearrange("(p t) k -> p (t k)", t=ROW_TILES)
@@ -55,25 +59,65 @@ def tile_persistentgrucell_pb_t_kernel(
     with ExitStack() as ctx:
         const = ctx.enter_context(tc.tile_pool(name="const", bufs=1))
         keep = ctx.enter_context(tc.tile_pool(name="keep", bufs=1))
-        loads = ctx.enter_context(tc.tile_pool(name="loads", bufs=LOAD_BUFS))
-        work = ctx.enter_context(tc.tile_pool(name="work", bufs=3))
+        outs = ctx.enter_context(tc.tile_pool(name="outs", bufs=10))
+        work = ctx.enter_context(tc.tile_pool(name="work", bufs=2))
         psum = ctx.enter_context(tc.psum_pool(name="psum", bufs=2))
         ctx.enter_context(tc.manual_schedule())
 
+        h_sb = {}
+        u_sb = {}
+        xr_words = {}
+
+        def load_h(c):
+            h_chunk = keep.tile([P, CHUNK_COLS], BF16, name="h_chunk%d" % c)
+            nc.sync.dma_start(out=h_chunk[:], in_=h_rows[:, c * CHUNK_COLS : (c + 1) * CHUNK_COLS])
+            h_sb[c] = h_chunk
+
+        def load_u(c):
+            u_chunk = keep.tile([P, CHUNK_COLS], BF16, name="u_chunk%d" % c)
+            nc.sync.dma_start(out=u_chunk[:], in_=u_rows[:, c * CHUNK_COLS : (c + 1) * CHUNK_COLS])
+            u_sb[c] = u_chunk
+
+        def load_xr(c):
+            xr_chunk = keep.tile([P, 2 * CHUNK_COLS], BF16, name="xr_chunk%d" % c)
+            xr_view = xr_chunk[:].rearrange("p (t j k) -> p t j k", j=2, k=H)
+            tiles = slice(c * CHUNK_TILES, (c + 1) * CHUNK_TILES)
+            nc.sync.dma_start(out=xr_view[:, :, 0, :], in_=x_rows[:, tiles, :])
+            nc.sync.dma_start(out=xr_view[:, :, 1, :], in_=rh_rows[:, tiles, :])
+            xr_words[c] = xr_chunk[:].bitcast(F32)
+
         vec_rows = const.tile([P, P], BF16)
         nc.vector.memset(vec_rows[:], 0.0)
+        decay_rows = const.tile([P, ONES_COLS], BF16)
+        nc.vector.memset(decay_rows[:], 0.0)
         for r, vec in enumerate((bn, connection_strength, connection_history)):
             nc.scalar.dma_start(
                 out=vec_rows[HALVES * r : HALVES * (r + 1), :],
                 in_=vec.rearrange("(a c) -> a c", a=HALVES),
             )
-        decay_bf16 = const.tile([P, 1], BF16)
-        nc.scalar.dma_start(out=decay_bf16[:], in_=connection_decay.partition_broadcast(P))
+        nc.scalar.dma_start(out=decay_rows[0:1, 0:1], in_=connection_decay.rearrange("(a c) -> a c", a=1))
+
+        load_h(0)
         w_sb = const.tile([P, HALVES * 2 * H], BF16)
         nc.sync.dma_start(
             out=w_sb[:].rearrange("p (a k) -> p a k", a=HALVES),
             in_=Wn.rearrange("(a p) k -> p a k", p=P),
         )
+        load_xr(0)
+        load_h(1)
+        load_h(2)
+        load_u(0)
+        load_xr(1)
+        load_h(3)
+        load_h(4)
+        load_u(1)
+        load_h(5)
+        load_h(6)
+        load_h(7)
+        for c in range(EARLY_CHUNKS, CHUNKS):
+            load_xr(c)
+            load_u(c)
+
         table_warm = const.tile([P, 1], F32)
         nc.vector.memset(table_warm[:], 0.0)
         nc.scalar.activation(out=table_warm[:], in_=table_warm[:], func=ACT.Tanh)
@@ -81,105 +125,112 @@ def tile_persistentgrucell_pb_t_kernel(
         make_identity(nc, ident_f32[:])
         ident_bf16 = const.tile([P, P], BF16)
         make_identity(nc, ident_bf16[:])
-        ones = const.tile([P, ONES_COLS], BF16)
+        neg_ident = const.tile([P, P], BF16)
+        nc.vector.tensor_scalar(
+            out=neg_ident[:], in0=ident_bf16[:], scalar1=-1.0, scalar2=None, op0=ALU.mult
+        )
+        ones = const.tile([P, P], BF16)
         nc.vector.memset(ones[:], 1.0)
 
-        w_words = w_sb[:].bitcast(F32)
-        wt_ps = psum.tile([P, 2, H], F32, tag="xt_ps")
-        for a in range(HALVES):
-            for s in range(2):
-                nc.tensor.transpose(
-                    wt_ps[:, s, a * P : (a + 1) * P],
-                    w_words[:, a * 2 * P + s : (a + 1) * 2 * P : 2],
-                    ident_f32[:],
-                )
-        w_grouped = const.tile([P, 4 * H], BF16, align_bytes=64)
-        nc.vector.tensor_copy(
-            out=w_grouped[:].bitcast(F32).rearrange("q (n s) -> q n s", s=2),
-            in_=wt_ps[:].rearrange("q s n -> q n s"),
-        )
-        w_codes = const.tile([P, H], U32, align_bytes=64)
-        w_scales = const.tile([P, H], U8, align_bytes=64)
-        nc.vector.quantize_mx(out=w_codes[:].bitcast(FP8X4), scales=w_scales[:], in_=w_grouped[:])
-
-        vec_ps = psum.tile([P, P], BF16, tag="acc_ps")
-        nc.tensor.transpose(vec_ps[:], vec_rows[:], ident_bf16[:])
-        vec_cols = const.tile([P, 3 * HALVES], F32)
-        nc.vector.tensor_copy(out=vec_cols[:], in_=vec_ps[:, 0 : 3 * HALVES])
-        bn_col = vec_cols[:, 0:HALVES]
-        strength_col = vec_cols[:, HALVES : 2 * HALVES]
-        history_col = vec_cols[:, 2 * HALVES : 3 * HALVES]
-        decay_col = const.tile([P, 1], F32)
-        nc.vector.tensor_copy(out=decay_col[:], in_=decay_bf16[:])
-        half_decayed = const.tile([P, HALVES], F32)
-        nc.vector.tensor_scalar(
-            out=half_decayed[:], in0=history_col, scalar1=decay_col[:, 0:1], scalar2=0.5, op0=ALU.mult, op1=ALU.mult
-        )
-        half_strength = const.tile([P, HALVES], F32)
-        nc.vector.tensor_scalar(out=half_strength[:], in0=strength_col, scalar1=0.5, scalar2=None, op0=ALU.mult)
-
         act_ps = [psum.tile([P, ONES_COLS], F32, tag="s_ps", bufs=4, name="act_ps%d" % a) for a in range(HALVES)]
-        u_sb = []
-        blend_sb = []
-        for c in range(CHUNKS):
-            chunk_cols = slice(c * CHUNK_COLS, (c + 1) * CHUNK_COLS)
-            h_chunk = keep.tile([P, CHUNK_COLS], BF16, name="h_chunk%d" % c)
-            nc.sync.dma_start(out=h_chunk[:], in_=h_rows[:, chunk_cols])
-            u_chunk = keep.tile([P, CHUNK_COLS], BF16, name="u_chunk%d" % c)
-            u_sb.append(u_chunk)
-            nc.sync.dma_start(out=u_chunk[:], in_=u_rows[:, chunk_cols])
+
+        def sum_abs(c):
             h_abs = work.tile([P, CHUNK_COLS], BF16)
-            nc.scalar.activation(out=h_abs[:], in_=h_chunk[:], func=ACT.Abs)
+            nc.vector.tensor_scalar(
+                out=h_abs[:].bitcast(I32),
+                in0=h_sb[c][:].bitcast(I32),
+                scalar1=SIGN_OFF,
+                scalar2=None,
+                op0=ALU.bitwise_and,
+            )
             blocks = CHUNK_COLS // P
             for k in range(blocks):
                 nc.tensor.matmul(
                     out=act_ps[k % HALVES][:],
                     lhsT=h_abs[:, k * P : (k + 1) * P],
-                    rhs=ones[:],
+                    rhs=ones[:, 0:ONES_COLS],
                     start=(c == 0 and k < HALVES),
                     stop=(c == CHUNKS - 1 and k >= blocks - HALVES),
                 )
-            blend_chunk = keep.tile([P, CHUNK_COLS], F32, name="blend_chunk%d" % c)
-            blend_sb.append(blend_chunk)
-            nc.vector.scalar_tensor_tensor(
-                out=blend_chunk[:],
-                in0=u_chunk[:],
-                scalar=1.0,
-                in1=h_chunk[:],
-                op0=ALU.subtract,
+
+        def prepare_weights():
+            w_words = w_sb[:].bitcast(F32)
+            wt_ps = psum.tile([P, 2, H], F32, tag="xt_ps")
+            for a in range(HALVES):
+                for s in range(2):
+                    nc.tensor.transpose(
+                        wt_ps[:, s, a * P : (a + 1) * P],
+                        w_words[:, a * 2 * P + s : (a + 1) * 2 * P : 2],
+                        ident_f32[:],
+                    )
+            w_grouped = const.tile([P, 4 * H], BF16, align_bytes=64)
+            nc.vector.tensor_copy(
+                out=w_grouped[:].bitcast(F32).rearrange("q (n s) -> q n s", s=2),
+                in_=wt_ps[:].rearrange("q s n -> q n s"),
+            )
+            w_codes = const.tile([P, H], U32, align_bytes=64)
+            w_scales = const.tile([P, H], U8, align_bytes=64)
+            nc.vector.quantize_mx(out=w_codes[:].bitcast(FP8X4), scales=w_scales[:], in_=w_grouped[:])
+            return w_codes, w_scales
+
+        def prepare_vectors():
+            vec_ps = psum.tile([P, P], BF16, tag="acc_ps")
+            nc.tensor.transpose(vec_ps[:], vec_rows[:], ident_bf16[:])
+            vec_cols = const.tile([P, 3 * HALVES], F32)
+            nc.vector.tensor_copy(out=vec_cols[:], in_=vec_ps[:, 0 : 3 * HALVES])
+            decay_ps = psum.tile([P, ONES_COLS], F32, tag="acc_ps")
+            nc.tensor.matmul(out=decay_ps[:], lhsT=ones[:], rhs=decay_rows[:], start=True, stop=True)
+            decay_col = const.tile([P, 1], F32)
+            nc.vector.tensor_copy(out=decay_col[:], in_=decay_ps[:, 0:1])
+            half_decayed = const.tile([P, HALVES], F32)
+            nc.vector.tensor_scalar(
+                out=half_decayed[:],
+                in0=vec_cols[:, 2 * HALVES : 3 * HALVES],
+                scalar1=decay_col[:, 0:1],
+                scalar2=0.5,
+                op0=ALU.mult,
                 op1=ALU.mult,
             )
-
-        tanh_col = const.tile([P, HALVES], F32)
-        for a in range(HALVES):
-            nc.scalar.activation(
-                out=tanh_col[:, a : a + 1],
-                in_=act_ps[a][:, 0:1],
-                func=ACT.Tanh,
-                bias=half_decayed[:, a : a + 1],
-                scale=0.5 / B,
+            half_strength = const.tile([P, HALVES], F32)
+            nc.vector.tensor_scalar(
+                out=half_strength[:],
+                in0=vec_cols[:, HALVES : 2 * HALVES],
+                scalar1=0.5,
+                scalar2=None,
+                op0=ALU.mult,
             )
-        cs_col = const.tile([P, HALVES], F32)
-        nc.vector.scalar_tensor_tensor(
-            out=cs_col[:], in0=tanh_col[:], scalar=1.0, in1=half_strength[:], op0=ALU.add, op1=ALU.mult
-        )
-        bias_col = const.tile([P, HALVES], F32)
-        nc.vector.tensor_tensor(out=bias_col[:], in0=bn_col, in1=cs_col[:], op=ALU.mult)
+            return vec_cols, half_decayed, half_strength
 
-        xr_words = {}
         grouped_of = {}
         codes_of = {}
         scales_of = {}
         scaled_of = {}
-        gated_of = {}
+        out_of = {}
 
-        def load_inputs(c):
-            chunk_cols = slice(c * CHUNK_COLS, (c + 1) * CHUNK_COLS)
-            xr_chunk = loads.tile([P, 2 * CHUNK_COLS], BF16)
-            xr_view = xr_chunk[:].rearrange("p (t j k) -> p t j k", j=2, k=H)
-            nc.sync.dma_start(out=xr_view[:, :, 0, :], in_=x_rows[:, chunk_cols].rearrange("p (t k) -> p t k", k=H))
-            nc.sync.dma_start(out=xr_view[:, :, 1, :], in_=rh_rows[:, chunk_cols].rearrange("p (t k) -> p t k", k=H))
-            xr_words[c] = xr_chunk[:].bitcast(F32)
+        def out_tile(g):
+            if g not in out_of:
+                out_group = outs.tile([P, GROUP_COLS], F32)
+                out_of[g] = out_group
+            return out_of[g]
+
+        def bank_cols(g, j):
+            c, gi = divmod(g, CHUNK_GROUPS)
+            lo = gi * GROUP_COLS + j * BANK_COLS
+            return c, slice(lo, lo + BANK_COLS)
+
+        def on_tensor(g, j):
+            return g >= EARLY_GROUPS and j == 0
+
+        def blend(g, j):
+            c, cols = bank_cols(g, j)
+            nc.vector.scalar_tensor_tensor(
+                out=out_tile(g)[:, j * BANK_COLS : (j + 1) * BANK_COLS],
+                in0=u_sb[c][:, cols],
+                scalar=1.0,
+                in1=h_sb[c][:, cols],
+                op0=ALU.subtract,
+                op1=ALU.mult,
+            )
 
         def transpose_inputs(g, j):
             c, gi = divmod(g, CHUNK_GROUPS)
@@ -202,8 +253,8 @@ def tile_persistentgrucell_pb_t_kernel(
             )
 
         def quantise(g):
-            codes = work.tile([P, GROUP_ROWS], U32, align_bytes=64)
-            scales = work.tile([P, GROUP_ROWS], U8, align_bytes=64)
+            codes = work.tile([P, GROUP_ROWS], U32, align_bytes=64, bufs=6)
+            scales = work.tile([P, GROUP_ROWS], U8, align_bytes=64, bufs=6)
             nc.vector.quantize_mx(out=codes[:].bitcast(FP8X4), scales=scales[:], in_=grouped_of[g][:])
             codes_of[g] = codes
             scales_of[g] = scales
@@ -230,51 +281,109 @@ def tile_persistentgrucell_pb_t_kernel(
                 )
             scaled_of[g] = scaled
 
+        gated_of = {}
+
         def gate_rows(g, j):
-            c, gi = divmod(g, CHUNK_GROUPS)
-            if j == 0:
-                gated = work.tile([P, GROUP_COLS], F32)
-                gated_of[g] = gated
-            s_ps = psum.tile([P, BANK_TILES * H], F32, bufs=4)
+            c, cols = bank_cols(g, j)
+            s_ps = psum.tile([P, BANK_COLS], F32, bufs=4)
+            if on_tensor(g, j):
+                nc.tensor.matmul(out=s_ps[:], lhsT=neg_ident[:], rhs=h_sb[c][:, cols], start=True, stop=False)
             for i in range(BANK_TILES):
                 n0 = (j * BANK_TILES + i) * P
                 for a in range(HALVES):
-                    block = s_ps[:, i * H + a * P : i * H + (a + 1) * P]
-                    if ((j * BANK_TILES + i) * HALVES + a) % MATMUL_EVERY == 0:
-                        nc.tensor.matmul(
-                            out=block, lhsT=scaled_of[g][:, a, n0 : n0 + P], rhs=ident_f32[:], start=True, stop=True
-                        )
-                    else:
-                        nc.tensor.transpose(block, scaled_of[g][:, a, n0 : n0 + P], ident_f32[:])
-            bank = slice(j * BANK_TILES * H, (j + 1) * BANK_TILES * H)
-            u_bank = slice(gi * GROUP_COLS + j * BANK_TILES * H, gi * GROUP_COLS + (j + 1) * BANK_TILES * H)
-            nc.vector.tensor_tensor(out=gated_of[g][:, bank], in0=s_ps[:], in1=u_sb[c][:, u_bank], op=ALU.mult)
+                    nc.tensor.matmul(
+                        out=s_ps[:, i * H + a * P : i * H + (a + 1) * P],
+                        lhsT=scaled_of[g][:, a, n0 : n0 + P],
+                        rhs=ident_f32[:],
+                        is_transpose=True,
+                        start=not on_tensor(g, j),
+                        stop=(not on_tensor(g, j)) or (i == BANK_TILES - 1 and a == HALVES - 1),
+                    )
+            if on_tensor(g, j):
+                gated = out_tile(g)[:, j * BANK_COLS : (j + 1) * BANK_COLS]
+            else:
+                gated_bank = work.tile([P, BANK_COLS], F32, bufs=4)
+                gated = gated_bank[:]
+            nc.vector.tensor_tensor(out=gated, in0=s_ps[:], in1=u_sb[c][:, cols], op=ALU.mult)
+            gated_of[g, j] = gated
 
-        def finish_rows(g):
-            c, gi = divmod(g, CHUNK_GROUPS)
-            group_cols = slice(gi * GROUP_COLS, (gi + 1) * GROUP_COLS)
-            split = GROUP_COLS - GPSIMD_TILES * H
-            for engine, lo, hi in ((nc.vector, 0, split), (nc.gpsimd, split, GROUP_COLS)):
-                cols = slice(gi * GROUP_COLS + lo, gi * GROUP_COLS + hi)
-                engine.tensor_tensor(
-                    out=blend_sb[c][:, cols], in0=gated_of[g][:, lo:hi], in1=blend_sb[c][:, cols], op=ALU.subtract
-                )
-            nc.sync.dma_start(out=out_rows[:, g * GROUP_COLS : (g + 1) * GROUP_COLS], in_=blend_sb[c][:, group_cols])
+        def finish_rows(g, j, engine):
+            c, cols = bank_cols(g, j)
+            out_bank = out_tile(g)[:, j * BANK_COLS : (j + 1) * BANK_COLS]
+            if on_tensor(g, j):
+                engine.tensor_tensor(out=out_bank, in0=out_bank, in1=h_sb[c][:, cols], op=ALU.add)
+            else:
+                engine.tensor_tensor(out=out_bank, in0=gated_of[g, j], in1=out_bank, op=ALU.subtract)
 
-        for c in range(LOAD_BUFS):
-            load_inputs(c)
-        for i in range(-3, GROUPS):
-            if 0 <= i + 1 < GROUPS:
+        def store(g, lo, hi):
+            nc.sync.dma_start(
+                out=out_rows[:, g * GROUP_COLS + lo * BANK_COLS : g * GROUP_COLS + hi * BANK_COLS],
+                in_=out_tile(g)[:, lo * BANK_COLS : hi * BANK_COLS],
+            )
+
+        def both_banks(step, g):
+            for j in range(GROUP_BANKS):
+                step(g, j)
+
+        sum_abs(0)
+        w_codes, w_scales = prepare_weights()
+        vec_cols, half_decayed, half_strength = prepare_vectors()
+        both_banks(transpose_inputs, 0)
+        both_banks(transpose_inputs, 1)
+        sum_abs(1)
+        quantise(0)
+        sum_abs(2)
+        quantise(1)
+        both_banks(blend, 0)
+        both_banks(blend, 1)
+        both_banks(transpose_inputs, 2)
+        both_banks(transpose_inputs, 3)
+        sum_abs(3)
+        quantise(2)
+        sum_abs(4)
+        quantise(3)
+        both_banks(blend, 2)
+        sum_abs(5)
+        sum_abs(6)
+        sum_abs(7)
+
+        tanh_col = const.tile([P, HALVES], F32)
+        for a in range(HALVES):
+            nc.scalar.activation(
+                out=tanh_col[:, a : a + 1],
+                in_=act_ps[a][:, 0:1],
+                func=ACT.Tanh,
+                bias=half_decayed[:, a : a + 1],
+                scale=0.5 / B,
+            )
+        cs_col = const.tile([P, HALVES], F32)
+        nc.vector.scalar_tensor_tensor(
+            out=cs_col[:], in0=tanh_col[:], scalar=1.0, in1=half_strength[:], op0=ALU.add, op1=ALU.mult
+        )
+        bias_col = const.tile([P, HALVES], F32)
+        nc.vector.tensor_tensor(out=bias_col[:], in0=vec_cols[:, 0:HALVES], in1=cs_col[:], op=ALU.mult)
+
+        multiply(0)
+        both_banks(blend, 3)
+        for i in range(GROUPS):
+            if i + 1 < GROUPS:
                 multiply(i + 1)
-            if 0 <= i + 2 < GROUPS:
-                quantise(i + 2)
-            for j in range(GROUP_TILES // BANK_TILES):
-                if 0 <= i:
-                    gate_rows(i, j)
-                if i + 3 < GROUPS:
-                    transpose_inputs(i + 3, j)
-            if 0 <= i:
-                finish_rows(i)
-            c, gi = divmod(i + 3, CHUNK_GROUPS)
-            if gi == CHUNK_GROUPS - 1 and c + LOAD_BUFS < CHUNKS:
-                load_inputs(c + LOAD_BUFS)
+            for j in range(GROUP_BANKS):
+                gate_rows(i, j)
+            ahead = i + EARLY_GROUPS
+            if ahead < GROUPS:
+                for j in range(GROUP_BANKS):
+                    transpose_inputs(ahead, j)
+            if EARLY_GROUPS <= ahead - 1 < GROUPS:
+                quantise(ahead - 1)
+            last = i == GROUPS - 1
+            if not on_tensor(i, 1) and i >= EARLY_GROUPS:
+                blend(i, 1)
+            finish_rows(i, 0, nc.vector)
+            if last:
+                store(i, 0, 1)
+                finish_rows(i, 1, nc.vector)
+                store(i, 1, 2)
+            else:
+                finish_rows(i, 1, nc.gpsimd)
+                store(i, 0, GROUP_BANKS)

@@ -28,8 +28,9 @@ CHUNK_GROUPS = 2
 CHUNK_TILES = CHUNK_GROUPS * GROUP_TILES
 CHUNK_COLS = CHUNK_GROUPS * GROUP_COLS
 CHUNKS = GROUPS // CHUNK_GROUPS
-EARLY_CHUNKS = 2
-EARLY_GROUPS = EARLY_CHUNKS * CHUNK_GROUPS
+AHEAD = 3
+BLENDED_GROUPS = 10
+EARLY_INPUT_GROUPS = AHEAD
 ONES_COLS = 2
 SIGN_OFF = 0x7FFF7FFF
 
@@ -78,13 +79,15 @@ def tile_persistentgrucell_pb_t_kernel(
             nc.sync.dma_start(out=u_chunk[:], in_=u_rows[:, c * CHUNK_COLS : (c + 1) * CHUNK_COLS])
             u_sb[c] = u_chunk
 
-        def load_xr(c):
-            xr_chunk = keep.tile([P, 2 * CHUNK_COLS], BF16, name="xr_chunk%d" % c)
+        def load_xr(lo, hi):
+            xr_chunk = keep.tile([P, 2 * (hi - lo) * GROUP_COLS], BF16, name="xr_chunk%d" % lo)
             xr_view = xr_chunk[:].rearrange("p (t j k) -> p t j k", j=2, k=H)
-            tiles = slice(c * CHUNK_TILES, (c + 1) * CHUNK_TILES)
+            tiles = slice(lo * GROUP_TILES, hi * GROUP_TILES)
             nc.sync.dma_start(out=xr_view[:, :, 0, :], in_=x_rows[:, tiles, :])
             nc.sync.dma_start(out=xr_view[:, :, 1, :], in_=rh_rows[:, tiles, :])
-            xr_words[c] = xr_chunk[:].bitcast(F32)
+            words = xr_chunk[:].bitcast(F32)
+            for g in range(lo, hi):
+                xr_words[g] = words[:, (g - lo) * GROUP_COLS : (g - lo + 1) * GROUP_COLS]
 
         vec_rows = const.tile([P, P], BF16)
         nc.vector.memset(vec_rows[:], 0.0)
@@ -103,20 +106,23 @@ def tile_persistentgrucell_pb_t_kernel(
             out=w_sb[:].rearrange("p (a k) -> p a k", a=HALVES),
             in_=Wn.rearrange("(a p) k -> p a k", p=P),
         )
-        load_xr(0)
-        load_h(1)
-        load_h(2)
         load_u(0)
-        load_xr(1)
-        load_h(3)
-        load_h(4)
+        load_h(1)
         load_u(1)
+        load_xr(0, EARLY_INPUT_GROUPS)
+        load_h(2)
+        load_u(2)
+        load_h(3)
+        load_u(3)
+        load_h(4)
         load_h(5)
+        load_u(4)
         load_h(6)
         load_h(7)
-        for c in range(EARLY_CHUNKS, CHUNKS):
-            load_xr(c)
-            load_u(c)
+        for g in range(EARLY_INPUT_GROUPS, GROUPS, CHUNK_GROUPS):
+            load_xr(g, min(g + CHUNK_GROUPS, GROUPS))
+            if g // CHUNK_GROUPS + 4 < CHUNKS:
+                load_u(g // CHUNK_GROUPS + 4)
 
         table_warm = const.tile([P, 1], F32)
         nc.vector.memset(table_warm[:], 0.0)
@@ -218,8 +224,8 @@ def tile_persistentgrucell_pb_t_kernel(
             lo = gi * GROUP_COLS + j * BANK_COLS
             return c, slice(lo, lo + BANK_COLS)
 
-        def on_tensor(g, j):
-            return g >= EARLY_GROUPS and j == 0
+        def on_tensor(g):
+            return g >= BLENDED_GROUPS
 
         def blend(g, j):
             c, cols = bank_cols(g, j)
@@ -233,18 +239,17 @@ def tile_persistentgrucell_pb_t_kernel(
             )
 
         def transpose_inputs(g, j):
-            c, gi = divmod(g, CHUNK_GROUPS)
             if j == 0:
                 grouped = work.tile([P, 4 * GROUP_ROWS], BF16, align_bytes=64)
                 grouped_of[g] = grouped
             grouped_words = grouped_of[g][:].bitcast(F32).rearrange("q (n s) -> q n s", s=2)
             xt_ps = psum.tile([P, 2, BANK_TILES * P], F32)
             for i in range(BANK_TILES):
-                t = gi * GROUP_TILES + j * BANK_TILES + i
+                t = j * BANK_TILES + i
                 for s in range(2):
                     nc.tensor.transpose(
                         xt_ps[:, s, i * P : (i + 1) * P],
-                        xr_words[c][:, t * 2 * P + s : (t + 1) * 2 * P : 2],
+                        xr_words[g][:, t * 2 * P + s : (t + 1) * 2 * P : 2],
                         ident_f32[:],
                     )
             nc.scalar.copy(
@@ -286,7 +291,7 @@ def tile_persistentgrucell_pb_t_kernel(
         def gate_rows(g, j):
             c, cols = bank_cols(g, j)
             s_ps = psum.tile([P, BANK_COLS], F32, bufs=4)
-            if on_tensor(g, j):
+            if on_tensor(g):
                 nc.tensor.matmul(out=s_ps[:], lhsT=neg_ident[:], rhs=h_sb[c][:, cols], start=True, stop=False)
             for i in range(BANK_TILES):
                 n0 = (j * BANK_TILES + i) * P
@@ -296,10 +301,10 @@ def tile_persistentgrucell_pb_t_kernel(
                         lhsT=scaled_of[g][:, a, n0 : n0 + P],
                         rhs=ident_f32[:],
                         is_transpose=True,
-                        start=not on_tensor(g, j),
-                        stop=(not on_tensor(g, j)) or (i == BANK_TILES - 1 and a == HALVES - 1),
+                        start=not on_tensor(g),
+                        stop=(not on_tensor(g)) or (i == BANK_TILES - 1 and a == HALVES - 1),
                     )
-            if on_tensor(g, j):
+            if on_tensor(g):
                 gated = out_tile(g)[:, j * BANK_COLS : (j + 1) * BANK_COLS]
             else:
                 gated_bank = work.tile([P, BANK_COLS], F32, bufs=4)
@@ -310,7 +315,7 @@ def tile_persistentgrucell_pb_t_kernel(
         def finish_rows(g, j, engine):
             c, cols = bank_cols(g, j)
             out_bank = out_tile(g)[:, j * BANK_COLS : (j + 1) * BANK_COLS]
-            if on_tensor(g, j):
+            if on_tensor(g):
                 engine.tensor_tensor(out=out_bank, in0=out_bank, in1=h_sb[c][:, cols], op=ALU.add)
             else:
                 engine.tensor_tensor(out=out_bank, in0=gated_of[g, j], in1=out_bank, op=ALU.subtract)
@@ -327,25 +332,25 @@ def tile_persistentgrucell_pb_t_kernel(
 
         sum_abs(0)
         w_codes, w_scales = prepare_weights()
-        vec_cols, half_decayed, half_strength = prepare_vectors()
-        both_banks(transpose_inputs, 0)
-        both_banks(transpose_inputs, 1)
-        sum_abs(1)
-        quantise(0)
-        sum_abs(2)
-        quantise(1)
         both_banks(blend, 0)
         both_banks(blend, 1)
-        both_banks(transpose_inputs, 2)
-        both_banks(transpose_inputs, 3)
-        sum_abs(3)
-        quantise(2)
-        sum_abs(4)
-        quantise(3)
+        vec_cols, half_decayed, half_strength = prepare_vectors()
+        sum_abs(1)
         both_banks(blend, 2)
-        sum_abs(5)
-        sum_abs(6)
-        sum_abs(7)
+        both_banks(blend, 3)
+        for g in range(EARLY_INPUT_GROUPS):
+            both_banks(transpose_inputs, g)
+        quantise(0)
+        sum_abs(2)
+        both_banks(blend, 4)
+        quantise(1)
+        both_banks(blend, 5)
+        sum_abs(3)
+        both_banks(blend, 6)
+        both_banks(blend, 7)
+        for c in range(4, CHUNKS):
+            sum_abs(c)
+        both_banks(blend, 8)
 
         tanh_col = const.tile([P, HALVES], F32)
         for a in range(HALVES):
@@ -364,23 +369,17 @@ def tile_persistentgrucell_pb_t_kernel(
         nc.vector.tensor_tensor(out=bias_col[:], in0=vec_cols[:, 0:HALVES], in1=cs_col[:], op=ALU.mult)
 
         multiply(0)
-        both_banks(blend, 3)
+        both_banks(blend, 9)
         for i in range(GROUPS):
             if i + 1 < GROUPS:
                 multiply(i + 1)
-            for j in range(GROUP_BANKS):
-                gate_rows(i, j)
-            ahead = i + EARLY_GROUPS
-            if ahead < GROUPS:
-                for j in range(GROUP_BANKS):
-                    transpose_inputs(ahead, j)
-            if EARLY_GROUPS <= ahead - 1 < GROUPS:
-                quantise(ahead - 1)
-            last = i == GROUPS - 1
-            if not on_tensor(i, 1) and i >= EARLY_GROUPS:
-                blend(i, 1)
+            if i + AHEAD - 1 < GROUPS:
+                quantise(i + AHEAD - 1)
+            both_banks(gate_rows, i)
+            if i + AHEAD < GROUPS:
+                both_banks(transpose_inputs, i + AHEAD)
             finish_rows(i, 0, nc.vector)
-            if last:
+            if i == GROUPS - 1:
                 store(i, 0, 1)
                 finish_rows(i, 1, nc.vector)
                 store(i, 1, 2)

@@ -28,8 +28,10 @@ CHUNK_GROUPS = 2
 CHUNK_TILES = CHUNK_GROUPS * GROUP_TILES
 CHUNK_COLS = CHUNK_GROUPS * GROUP_COLS
 CHUNKS = GROUPS // CHUNK_GROUPS
-AHEAD = 3
-BLENDED_GROUPS = 10
+AHEAD = 4
+BLENDED_CHUNKS = 5
+BLENDED_GROUPS = BLENDED_CHUNKS * CHUNK_GROUPS
+ORDERED_GROUPS = 6
 EARLY_INPUT_GROUPS = AHEAD
 ONES_COLS = 2
 SIGN_OFF = 0x7FFF7FFF
@@ -60,7 +62,7 @@ def tile_persistentgrucell_pb_t_kernel(
     with ExitStack() as ctx:
         const = ctx.enter_context(tc.tile_pool(name="const", bufs=1))
         keep = ctx.enter_context(tc.tile_pool(name="keep", bufs=1))
-        outs = ctx.enter_context(tc.tile_pool(name="outs", bufs=10))
+        outs = ctx.enter_context(tc.tile_pool(name="outs", bufs=11))
         work = ctx.enter_context(tc.tile_pool(name="work", bufs=2))
         psum = ctx.enter_context(tc.psum_pool(name="psum", bufs=2))
         ctx.enter_context(tc.manual_schedule())
@@ -68,6 +70,9 @@ def tile_persistentgrucell_pb_t_kernel(
         h_sb = {}
         u_sb = {}
         xr_words = {}
+        raw_words = {}
+        x_flat = x.rearrange("(p t) k -> p (t k)", t=ROW_TILES)
+        rh_flat = rh.rearrange("(p t) k -> p (t k)", t=ROW_TILES)
 
         def load_h(c):
             h_chunk = keep.tile([P, CHUNK_COLS], BF16, name="h_chunk%d" % c)
@@ -80,6 +85,16 @@ def tile_persistentgrucell_pb_t_kernel(
             u_sb[c] = u_chunk
 
         def load_xr(lo, hi):
+            if lo < ORDERED_GROUPS:
+                cols = slice(lo * GROUP_COLS, hi * GROUP_COLS)
+                x_chunk = keep.tile([P, (hi - lo) * GROUP_COLS], BF16, name="x_chunk%d" % lo)
+                nc.sync.dma_start(out=x_chunk[:], in_=x_flat[:, cols])
+                rh_chunk = keep.tile([P, (hi - lo) * GROUP_COLS], BF16, name="rh_chunk%d" % lo)
+                nc.sync.dma_start(out=rh_chunk[:], in_=rh_flat[:, cols])
+                for g in range(lo, hi):
+                    cols = slice((g - lo) * GROUP_COLS, (g - lo + 1) * GROUP_COLS)
+                    raw_words[g] = (x_chunk[:, cols].bitcast(F32), rh_chunk[:, cols].bitcast(F32))
+                return
             xr_chunk = keep.tile([P, 2 * (hi - lo) * GROUP_COLS], BF16, name="xr_chunk%d" % lo)
             xr_view = xr_chunk[:].rearrange("p (t j k) -> p t j k", j=2, k=H)
             tiles = slice(lo * GROUP_TILES, hi * GROUP_TILES)
@@ -93,13 +108,6 @@ def tile_persistentgrucell_pb_t_kernel(
         nc.vector.memset(vec_rows[:], 0.0)
         decay_rows = const.tile([P, ONES_COLS], BF16)
         nc.vector.memset(decay_rows[:], 0.0)
-        for r, vec in enumerate((bn, connection_strength, connection_history)):
-            nc.scalar.dma_start(
-                out=vec_rows[HALVES * r : HALVES * (r + 1), :],
-                in_=vec.rearrange("(a c) -> a c", a=HALVES),
-            )
-        nc.scalar.dma_start(out=decay_rows[0:1, 0:1], in_=connection_decay.rearrange("(a c) -> a c", a=1))
-
         load_h(0)
         w_sb = const.tile([P, HALVES * 2 * H], BF16)
         nc.sync.dma_start(
@@ -109,20 +117,26 @@ def tile_persistentgrucell_pb_t_kernel(
         load_u(0)
         load_h(1)
         load_u(1)
-        load_xr(0, EARLY_INPUT_GROUPS)
         load_h(2)
         load_u(2)
+        load_xr(0, 2)
         load_h(3)
         load_u(3)
+        load_xr(2, 4)
         load_h(4)
         load_h(5)
-        load_u(4)
         load_h(6)
         load_h(7)
-        for g in range(EARLY_INPUT_GROUPS, GROUPS, CHUNK_GROUPS):
-            load_xr(g, min(g + CHUNK_GROUPS, GROUPS))
-            if g // CHUNK_GROUPS + 4 < CHUNKS:
-                load_u(g // CHUNK_GROUPS + 4)
+        load_u(4)
+        load_xr(4, 6)
+        load_xr(6, 8)
+        load_u(5)
+        load_xr(8, 10)
+        load_u(6)
+        load_xr(10, 12)
+        load_u(7)
+        load_xr(12, 14)
+        load_xr(14, 16)
 
         table_warm = const.tile([P, 1], F32)
         nc.vector.memset(table_warm[:], 0.0)
@@ -131,6 +145,12 @@ def tile_persistentgrucell_pb_t_kernel(
         make_identity(nc, ident_f32[:])
         ident_bf16 = const.tile([P, P], BF16)
         make_identity(nc, ident_bf16[:])
+        for r, vec in enumerate((bn, connection_strength, connection_history)):
+            nc.gpsimd.dma_start(
+                out=vec_rows[HALVES * r : HALVES * (r + 1), :],
+                in_=vec.rearrange("(a c) -> a c", a=HALVES),
+            )
+        nc.gpsimd.dma_start(out=decay_rows[0:1, 0:1], in_=connection_decay.rearrange("(a c) -> a c", a=1))
         neg_ident = const.tile([P, P], BF16)
         nc.vector.tensor_scalar(
             out=neg_ident[:], in0=ident_bf16[:], scalar1=-1.0, scalar2=None, op0=ALU.mult
@@ -238,9 +258,18 @@ def tile_persistentgrucell_pb_t_kernel(
                 op1=ALU.mult,
             )
 
+        ordered_of = {}
+
+        def order_words(g):
+            ordered = work.tile([P, GROUP_COLS], F32, bufs=2)
+            view = ordered[:].rearrange("p (t s j w) -> p t j w s", s=2, j=2, w=H // 4)
+            for n, words in enumerate(raw_words[g]):
+                nc.scalar.copy(out=view[:, :, n, :, :], in_=words.rearrange("p (t w s) -> p t w s", s=2, w=H // 4))
+            ordered_of[g] = ordered
+
         def transpose_inputs(g, j):
             if j == 0:
-                grouped = work.tile([P, 4 * GROUP_ROWS], BF16, align_bytes=64)
+                grouped = work.tile([P, 4 * GROUP_ROWS], BF16, align_bytes=64, bufs=3)
                 grouped_of[g] = grouped
             grouped_words = grouped_of[g][:].bitcast(F32).rearrange("q (n s) -> q n s", s=2)
             xt_ps = psum.tile([P, 2, BANK_TILES * P], F32)
@@ -249,7 +278,9 @@ def tile_persistentgrucell_pb_t_kernel(
                 for s in range(2):
                     nc.tensor.transpose(
                         xt_ps[:, s, i * P : (i + 1) * P],
-                        xr_words[g][:, t * 2 * P + s : (t + 1) * 2 * P : 2],
+                        xr_words[g][:, t * 2 * P + s : (t + 1) * 2 * P : 2]
+                        if g >= ORDERED_GROUPS
+                        else ordered_of[g][:, (t * 2 + s) * P : (t * 2 + s + 1) * P],
                         ident_f32[:],
                     )
             nc.scalar.copy(
@@ -258,8 +289,8 @@ def tile_persistentgrucell_pb_t_kernel(
             )
 
         def quantise(g):
-            codes = work.tile([P, GROUP_ROWS], U32, align_bytes=64, bufs=6)
-            scales = work.tile([P, GROUP_ROWS], U8, align_bytes=64, bufs=6)
+            codes = work.tile([P, GROUP_ROWS], U32, align_bytes=64, bufs=4)
+            scales = work.tile([P, GROUP_ROWS], U8, align_bytes=64, bufs=4)
             nc.vector.quantize_mx(out=codes[:].bitcast(FP8X4), scales=scales[:], in_=grouped_of[g][:])
             codes_of[g] = codes
             scales_of[g] = scales
@@ -338,19 +369,26 @@ def tile_persistentgrucell_pb_t_kernel(
         sum_abs(1)
         both_banks(blend, 2)
         both_banks(blend, 3)
-        for g in range(EARLY_INPUT_GROUPS):
-            both_banks(transpose_inputs, g)
-        quantise(0)
         sum_abs(2)
         both_banks(blend, 4)
-        quantise(1)
         both_banks(blend, 5)
+        order_words(0)
+        order_words(1)
+        both_banks(transpose_inputs, 0)
+        both_banks(transpose_inputs, 1)
         sum_abs(3)
+        order_words(2)
+        order_words(3)
         both_banks(blend, 6)
+        quantise(0)
         both_banks(blend, 7)
-        for c in range(4, CHUNKS):
-            sum_abs(c)
-        both_banks(blend, 8)
+        both_banks(transpose_inputs, 2)
+        both_banks(transpose_inputs, 3)
+        quantise(1)
+        sum_abs(4)
+        sum_abs(5)
+        sum_abs(6)
+        sum_abs(7)
 
         tanh_col = const.tile([P, HALVES], F32)
         for a in range(HALVES):
@@ -369,15 +407,20 @@ def tile_persistentgrucell_pb_t_kernel(
         nc.vector.tensor_tensor(out=bias_col[:], in0=vec_cols[:, 0:HALVES], in1=cs_col[:], op=ALU.mult)
 
         multiply(0)
+        both_banks(blend, 8)
         both_banks(blend, 9)
+        order_words(4)
+
         for i in range(GROUPS):
             if i + 1 < GROUPS:
                 multiply(i + 1)
-            if i + AHEAD - 1 < GROUPS:
-                quantise(i + AHEAD - 1)
+            if i + 2 < GROUPS:
+                quantise(i + 2)
             both_banks(gate_rows, i)
             if i + AHEAD < GROUPS:
                 both_banks(transpose_inputs, i + AHEAD)
+            if i + AHEAD + 1 < ORDERED_GROUPS:
+                order_words(i + AHEAD + 1)
             finish_rows(i, 0, nc.vector)
             if i == GROUPS - 1:
                 store(i, 0, 1)

@@ -108,6 +108,12 @@ def tile_persistentgrucell_pb_t_kernel(
         nc.vector.memset(vec_rows[:], 0.0)
         decay_rows = const.tile([P, ONES_COLS], BF16)
         nc.vector.memset(decay_rows[:], 0.0)
+        for r, vec in enumerate((bn, connection_strength, connection_history)):
+            nc.scalar.dma_start(
+                out=vec_rows[HALVES * r : HALVES * (r + 1), :],
+                in_=vec.rearrange("(a c) -> a c", a=HALVES),
+            )
+        nc.scalar.dma_start(out=decay_rows[0:1, 0:1], in_=connection_decay.rearrange("(a c) -> a c", a=1))
         load_h(0)
         w_sb = const.tile([P, HALVES * 2 * H], BF16)
         nc.sync.dma_start(
@@ -145,12 +151,6 @@ def tile_persistentgrucell_pb_t_kernel(
         make_identity(nc, ident_f32[:])
         ident_bf16 = const.tile([P, P], BF16)
         make_identity(nc, ident_bf16[:])
-        for r, vec in enumerate((bn, connection_strength, connection_history)):
-            nc.gpsimd.dma_start(
-                out=vec_rows[HALVES * r : HALVES * (r + 1), :],
-                in_=vec.rearrange("(a c) -> a c", a=HALVES),
-            )
-        nc.gpsimd.dma_start(out=decay_rows[0:1, 0:1], in_=connection_decay.rearrange("(a c) -> a c", a=1))
         neg_ident = const.tile([P, P], BF16)
         nc.vector.tensor_scalar(
             out=neg_ident[:], in0=ident_bf16[:], scalar1=-1.0, scalar2=None, op0=ALU.mult
@@ -363,9 +363,9 @@ def tile_persistentgrucell_pb_t_kernel(
 
         sum_abs(0)
         w_codes, w_scales = prepare_weights()
+        vec_cols, half_decayed, half_strength = prepare_vectors()
         both_banks(blend, 0)
         both_banks(blend, 1)
-        vec_cols, half_decayed, half_strength = prepare_vectors()
         sum_abs(1)
         both_banks(blend, 2)
         both_banks(blend, 3)

@@ -31,7 +31,7 @@ CHUNKS = GROUPS // CHUNK_GROUPS
 AHEAD = 4
 BLENDED_CHUNKS = 5
 BLENDED_GROUPS = BLENDED_CHUNKS * CHUNK_GROUPS
-ORDERED_GROUPS = 6
+ORDERED_GROUPS = 4
 EARLY_INPUT_GROUPS = AHEAD
 ONES_COLS = 2
 SIGN_OFF = 0x7FFF7FFF
@@ -158,10 +158,10 @@ def tile_persistentgrucell_pb_t_kernel(
         ones = const.tile([P, P], BF16)
         nc.vector.memset(ones[:], 1.0)
 
-        act_ps = [psum.tile([P, ONES_COLS], F32, tag="s_ps", bufs=4, name="act_ps%d" % a) for a in range(HALVES)]
+        act_ps = [psum.tile([P, ONES_COLS], F32, tag="s_ps", bufs=3, name="act_ps%d" % a) for a in range(HALVES)]
 
         def sum_abs(c):
-            h_abs = work.tile([P, CHUNK_COLS], BF16)
+            h_abs = work.tile([P, CHUNK_COLS], BF16, bufs=3)
             nc.vector.tensor_scalar(
                 out=h_abs[:].bitcast(I32),
                 in0=h_sb[c][:].bitcast(I32),
@@ -200,11 +200,11 @@ def tile_persistentgrucell_pb_t_kernel(
             return w_codes, w_scales
 
         def prepare_vectors():
-            vec_ps = psum.tile([P, P], BF16, tag="acc_ps")
+            vec_ps = psum.tile([P, P], BF16, tag="acc_ps", bufs=3)
             nc.tensor.transpose(vec_ps[:], vec_rows[:], ident_bf16[:])
             vec_cols = const.tile([P, 3 * HALVES], F32)
             nc.vector.tensor_copy(out=vec_cols[:], in_=vec_ps[:, 0 : 3 * HALVES])
-            decay_ps = psum.tile([P, ONES_COLS], F32, tag="acc_ps")
+            decay_ps = psum.tile([P, ONES_COLS], F32, tag="acc_ps", bufs=3)
             nc.tensor.matmul(out=decay_ps[:], lhsT=ones[:], rhs=decay_rows[:], start=True, stop=True)
             decay_col = const.tile([P, 1], F32)
             nc.vector.tensor_copy(out=decay_col[:], in_=decay_ps[:, 0:1])
@@ -225,7 +225,9 @@ def tile_persistentgrucell_pb_t_kernel(
                 scalar2=None,
                 op0=ALU.mult,
             )
-            return vec_cols, half_decayed, half_strength
+            half_strength_bn = const.tile([P, HALVES], F32)
+            nc.vector.tensor_tensor(out=half_strength_bn[:], in0=half_strength[:], in1=vec_cols[:, 0:HALVES], op=ALU.mult)
+            return half_strength_bn, half_decayed, half_strength
 
         grouped_of = {}
         codes_of = {}
@@ -298,7 +300,7 @@ def tile_persistentgrucell_pb_t_kernel(
         def multiply(g):
             scaled = work.tile([P, HALVES, GROUP_ROWS], F32)
             for a in range(HALVES):
-                acc_ps = psum.tile([P, GROUP_ROWS], F32)
+                acc_ps = psum.tile([P, GROUP_ROWS], F32, bufs=3)
                 nc.tensor.matmul_mx(
                     out=acc_ps[:],
                     lhsT=w_codes[:, a * P : (a + 1) * P].bitcast(FP8X4),
@@ -321,7 +323,7 @@ def tile_persistentgrucell_pb_t_kernel(
 
         def gate_rows(g, j):
             c, cols = bank_cols(g, j)
-            s_ps = psum.tile([P, BANK_COLS], F32, bufs=4)
+            s_ps = psum.tile([P, BANK_COLS], F32, bufs=3)
             if on_tensor(g):
                 nc.tensor.matmul(out=s_ps[:], lhsT=neg_ident[:], rhs=h_sb[c][:, cols], start=True, stop=False)
             for i in range(BANK_TILES):
@@ -343,13 +345,13 @@ def tile_persistentgrucell_pb_t_kernel(
             nc.vector.tensor_tensor(out=gated, in0=s_ps[:], in1=u_sb[c][:, cols], op=ALU.mult)
             gated_of[g, j] = gated
 
-        def finish_rows(g, j, engine):
+        def finish_rows(g, j, engine, lo=0, hi=BANK_COLS):
             c, cols = bank_cols(g, j)
-            out_bank = out_tile(g)[:, j * BANK_COLS : (j + 1) * BANK_COLS]
+            out_bank = out_tile(g)[:, j * BANK_COLS + lo : j * BANK_COLS + hi]
             if on_tensor(g):
-                engine.tensor_tensor(out=out_bank, in0=out_bank, in1=h_sb[c][:, cols], op=ALU.add)
+                engine.tensor_tensor(out=out_bank, in0=out_bank, in1=h_sb[c][:, cols][:, lo:hi], op=ALU.add)
             else:
-                engine.tensor_tensor(out=out_bank, in0=gated_of[g, j], in1=out_bank, op=ALU.subtract)
+                engine.tensor_tensor(out=out_bank, in0=gated_of[g, j][:, lo:hi], in1=out_bank, op=ALU.subtract)
 
         def store(g, lo, hi):
             nc.sync.dma_start(
@@ -363,7 +365,7 @@ def tile_persistentgrucell_pb_t_kernel(
 
         sum_abs(0)
         w_codes, w_scales = prepare_weights()
-        vec_cols, half_decayed, half_strength = prepare_vectors()
+        half_strength_bn, half_decayed, half_strength = prepare_vectors()
         both_banks(blend, 0)
         both_banks(blend, 1)
         sum_abs(1)
@@ -382,12 +384,12 @@ def tile_persistentgrucell_pb_t_kernel(
         both_banks(blend, 6)
         quantise(0)
         both_banks(blend, 7)
-        both_banks(transpose_inputs, 2)
-        both_banks(transpose_inputs, 3)
         quantise(1)
         sum_abs(4)
         sum_abs(5)
+        both_banks(transpose_inputs, 2)
         sum_abs(6)
+        both_banks(transpose_inputs, 3)
         sum_abs(7)
 
         tanh_col = const.tile([P, HALVES], F32)
@@ -404,12 +406,13 @@ def tile_persistentgrucell_pb_t_kernel(
             out=cs_col[:], in0=tanh_col[:], scalar=1.0, in1=half_strength[:], op0=ALU.add, op1=ALU.mult
         )
         bias_col = const.tile([P, HALVES], F32)
-        nc.vector.tensor_tensor(out=bias_col[:], in0=vec_cols[:, 0:HALVES], in1=cs_col[:], op=ALU.mult)
+        nc.vector.scalar_tensor_tensor(
+            out=bias_col[:], in0=tanh_col[:], scalar=1.0, in1=half_strength_bn[:], op0=ALU.add, op1=ALU.mult
+        )
 
         multiply(0)
         both_banks(blend, 8)
         both_banks(blend, 9)
-        order_words(4)
 
         for i in range(GROUPS):
             if i + 1 < GROUPS:
@@ -427,5 +430,6 @@ def tile_persistentgrucell_pb_t_kernel(
                 finish_rows(i, 1, nc.vector)
                 store(i, 1, 2)
             else:
-                finish_rows(i, 1, nc.gpsimd)
+                finish_rows(i, 1, nc.vector, 0, 128)
+                finish_rows(i, 1, nc.gpsimd, 128)
                 store(i, 0, GROUP_BANKS)

@@ -383,13 +383,12 @@ def tile_persistentgrucell_pb_t_kernel(
         order_words(3)
         both_banks(blend, 6)
         quantise(0)
+        both_banks(transpose_inputs, 2)
         both_banks(blend, 7)
         quantise(1)
         sum_abs(4)
         sum_abs(5)
-        both_banks(transpose_inputs, 2)
         sum_abs(6)
-        both_banks(transpose_inputs, 3)
         sum_abs(7)
 
         tanh_col = const.tile([P, HALVES], F32)
@@ -411,6 +410,7 @@ def tile_persistentgrucell_pb_t_kernel(
         )
 
         multiply(0)
+        both_banks(transpose_inputs, 3)
         both_banks(blend, 8)
         both_banks(blend, 9)
 

@@ -342,7 +342,7 @@ def tile_persistentgrucell_pb_t_kernel(
             else:
                 gated_bank = work.tile([P, BANK_COLS], F32, bufs=4)
                 gated = gated_bank[:]
-            nc.vector.tensor_tensor(out=gated, in0=s_ps[:], in1=u_sb[c][:, cols], op=ALU.mult)
+            nc.vector.tensor_tensor(out=gated, in0=u_sb[c][:, cols], in1=s_ps[:], op=ALU.mult)
             gated_of[g, j] = gated
 
         def finish_rows(g, j, engine, lo=0, hi=BANK_COLS):

from contextlib import ExitStack

import concourse.mybir as mybir
from concourse.masks import make_identity

F32 = mybir.dt.float32
BF16 = mybir.dt.bfloat16
I32 = mybir.dt.int32
U32 = mybir.dt.uint32
U8 = mybir.dt.uint8
FP8X4 = mybir.dt.float8_e4m3fn_x4
ALU = mybir.AluOpType
ACT = mybir.ActivationFunctionType

P = 128
B = 8192
H = 256
HALVES = H // P
ROW_TILES = B // P
BANK_TILES = 2
BANK_COLS = BANK_TILES * H
GROUP_TILES = 4
GROUP_BANKS = GROUP_TILES // BANK_TILES
GROUP_ROWS = GROUP_TILES * P
GROUP_COLS = GROUP_TILES * H
GROUPS = ROW_TILES // GROUP_TILES
CHUNK_GROUPS = 2
CHUNK_TILES = CHUNK_GROUPS * GROUP_TILES
CHUNK_COLS = CHUNK_GROUPS * GROUP_COLS
CHUNKS = GROUPS // CHUNK_GROUPS
AHEAD = 4
BLENDED_CHUNKS = 5
BLENDED_GROUPS = BLENDED_CHUNKS * CHUNK_GROUPS
ORDERED_GROUPS = 4
EARLY_INPUT_GROUPS = AHEAD
ONES_COLS = 2
SIGN_OFF = 0x7FFF7FFF

FLOPS = 2 * B * (2 * H) * H


def tile_persistentgrucell_pb_t_kernel(
    tc,
    x,
    rh,
    update,
    hidden,
    Wn,
    bn,
    connection_strength,
    connection_decay,
    connection_history,
    out,
):
    nc = tc.nc
    x_rows = x.rearrange("(p t) k -> p t k", t=ROW_TILES)
    rh_rows = rh.rearrange("(p t) k -> p t k", t=ROW_TILES)
    u_rows = update.rearrange("(p t) k -> p (t k)", t=ROW_TILES)
    h_rows = hidden.rearrange("(p t) k -> p (t k)", t=ROW_TILES)
    out_rows = out.rearrange("(p t) k -> p (t k)", t=ROW_TILES)

    with ExitStack() as ctx:
        const = ctx.enter_context(tc.tile_pool(name="const", bufs=1))
        keep = ctx.enter_context(tc.tile_pool(name="keep", bufs=1))
        outs = ctx.enter_context(tc.tile_pool(name="outs", bufs=11))
        work = ctx.enter_context(tc.tile_pool(name="work", bufs=2))
        psum = ctx.enter_context(tc.psum_pool(name="psum", bufs=2))
        ctx.enter_context(tc.manual_schedule())

        h_sb = {}
        u_sb = {}
        xr_words = {}
        raw_words = {}
        x_flat = x.rearrange("(p t) k -> p (t k)", t=ROW_TILES)
        rh_flat = rh.rearrange("(p t) k -> p (t k)", t=ROW_TILES)

        def load_h(c):
            h_chunk = keep.tile([P, CHUNK_COLS], BF16, name="h_chunk%d" % c)
            nc.sync.dma_start(out=h_chunk[:], in_=h_rows[:, c * CHUNK_COLS : (c + 1) * CHUNK_COLS])
            h_sb[c] = h_chunk

        def load_u(c):
            u_chunk = keep.tile([P, CHUNK_COLS], BF16, name="u_chunk%d" % c)
            nc.sync.dma_start(out=u_chunk[:], in_=u_rows[:, c * CHUNK_COLS : (c + 1) * CHUNK_COLS])
            u_sb[c] = u_chunk

        def load_xr(lo, hi):
            if lo < ORDERED_GROUPS:
                cols = slice(lo * GROUP_COLS, hi * GROUP_COLS)
                x_chunk = keep.tile([P, (hi - lo) * GROUP_COLS], BF16, name="x_chunk%d" % lo)
                nc.sync.dma_start(out=x_chunk[:], in_=x_flat[:, cols])
                rh_chunk = keep.tile([P, (hi - lo) * GROUP_COLS], BF16, name="rh_chunk%d" % lo)
                nc.sync.dma_start(out=rh_chunk[:], in_=rh_flat[:, cols])
                for g in range(lo, hi):
                    cols = slice((g - lo) * GROUP_COLS, (g - lo + 1) * GROUP_COLS)
                    raw_words[g] = (x_chunk[:, cols].bitcast(F32), rh_chunk[:, cols].bitcast(F32))
                return
            xr_chunk = keep.tile([P, 2 * (hi - lo) * GROUP_COLS], BF16, name="xr_chunk%d" % lo)
            xr_view = xr_chunk[:].rearrange("p (t j k) -> p t j k", j=2, k=H)
            tiles = slice(lo * GROUP_TILES, hi * GROUP_TILES)
            nc.sync.dma_start(out=xr_view[:, :, 0, :], in_=x_rows[:, tiles, :])
            nc.sync.dma_start(out=xr_view[:, :, 1, :], in_=rh_rows[:, tiles, :])
            words = xr_chunk[:].bitcast(F32)
            for g in range(lo, hi):
                xr_words[g] = words[:, (g - lo) * GROUP_COLS : (g - lo + 1) * GROUP_COLS]

        vec_rows = const.tile([P, P], BF16)
        nc.vector.memset(vec_rows[:], 0.0)
        decay_rows = const.tile([P, ONES_COLS], BF16)
        nc.vector.memset(decay_rows[:], 0.0)
        for r, vec in enumerate((bn, connection_strength, connection_history)):
            nc.scalar.dma_start(
                out=vec_rows[HALVES * r : HALVES * (r + 1), :],
                in_=vec.rearrange("(a c) -> a c", a=HALVES),
            )
        nc.scalar.dma_start(out=decay_rows[0:1, 0:1], in_=connection_decay.rearrange("(a c) -> a c", a=1))
        load_h(0)
        w_sb = const.tile([P, HALVES * 2 * H], BF16)
        nc.sync.dma_start(
            out=w_sb[:].rearrange("p (a k) -> p a k", a=HALVES),
            in_=Wn.rearrange("(a p) k -> p a k", p=P),
        )
        load_u(0)
        load_h(1)
        load_u(1)
        load_h(2)
        load_u(2)
        load_xr(0, 2)
        load_h(3)
        load_u(3)
        load_xr(2, 4)
        load_h(4)
        load_h(5)
        load_h(6)
        load_h(7)
        load_u(4)
        load_xr(4, 6)
        load_xr(6, 8)
        load_u(5)
        load_xr(8, 10)
        load_u(6)
        load_xr(10, 12)
        load_u(7)
        load_xr(12, 14)
        load_xr(14, 16)

        table_warm = const.tile([P, 1], F32)
        nc.vector.memset(table_warm[:], 0.0)
        nc.scalar.activation(out=table_warm[:], in_=table_warm[:], func=ACT.Tanh)
        ident_f32 = const.tile([P, P], F32)
        make_identity(nc, ident_f32[:])
        ident_bf16 = const.tile([P, P], BF16)
        make_identity(nc, ident_bf16[:])
        neg_ident = const.tile([P, P], BF16)
        nc.vector.tensor_scalar(
            out=neg_ident[:], in0=ident_bf16[:], scalar1=-1.0, scalar2=None, op0=ALU.mult
        )
        ones = const.tile([P, P], BF16)
        nc.vector.memset(ones[:], 1.0)

        act_ps = [psum.tile([P, ONES_COLS], F32, tag="s_ps", bufs=3, name="act_ps%d" % a) for a in range(HALVES)]

        def sum_abs(c):
            h_abs = work.tile([P, CHUNK_COLS], BF16, bufs=3)
            nc.vector.tensor_scalar(
                out=h_abs[:].bitcast(I32),
                in0=h_sb[c][:].bitcast(I32),
                scalar1=SIGN_OFF,
                scalar2=None,
                op0=ALU.bitwise_and,
            )
            blocks = CHUNK_COLS // P
            for k in range(blocks):
                nc.tensor.matmul(
                    out=act_ps[k % HALVES][:],
                    lhsT=h_abs[:, k * P : (k + 1) * P],
                    rhs=ones[:, 0:ONES_COLS],
                    start=(c == 0 and k < HALVES),
                    stop=(c == CHUNKS - 1 and k >= blocks - HALVES),
                )

        def prepare_weights():
            w_words = w_sb[:].bitcast(F32)
            wt_ps = psum.tile([P, 2, H], F32, tag="xt_ps")
            for a in range(HALVES):
                for s in range(2):
                    nc.tensor.transpose(
                        wt_ps[:, s, a * P : (a + 1) * P],
                        w_words[:, a * 2 * P + s : (a + 1) * 2 * P : 2],
                        ident_f32[:],
                    )
            w_grouped = const.tile([P, 4 * H], BF16, align_bytes=64)
            nc.vector.tensor_copy(
                out=w_grouped[:].bitcast(F32).rearrange("q (n s) -> q n s", s=2),
                in_=wt_ps[:].rearrange("q s n -> q n s"),
            )
            w_codes = const.tile([P, H], U32, align_bytes=64)
            w_scales = const.tile([P, H], U8, align_bytes=64)
            nc.vector.quantize_mx(out=w_codes[:].bitcast(FP8X4), scales=w_scales[:], in_=w_grouped[:])
            return w_codes, w_scales

        def prepare_vectors():
            vec_ps = psum.tile([P, P], BF16, tag="acc_ps", bufs=3)
            nc.tensor.transpose(vec_ps[:], vec_rows[:], ident_bf16[:])
            vec_cols = const.tile([P, 3 * HALVES], F32)
            nc.vector.tensor_copy(out=vec_cols[:], in_=vec_ps[:, 0 : 3 * HALVES])
            decay_ps = psum.tile([P, ONES_COLS], F32, tag="acc_ps", bufs=3)
            nc.tensor.matmul(out=decay_ps[:], lhsT=ones[:], rhs=decay_rows[:], start=True, stop=True)
            decay_col = const.tile([P, 1], F32)
            nc.vector.tensor_copy(out=decay_col[:], in_=decay_ps[:, 0:1])
            half_decayed = const.tile([P, HALVES], F32)
            nc.vector.tensor_scalar(
                out=half_decayed[:],
                in0=vec_cols[:, 2 * HALVES : 3 * HALVES],
                scalar1=decay_col[:, 0:1],
                scalar2=0.5,
                op0=ALU.mult,
                op1=ALU.mult,
            )
            half_strength = const.tile([P, HALVES], F32)
            nc.vector.tensor_scalar(
                out=half_strength[:],
                in0=vec_cols[:, HALVES : 2 * HALVES],
                scalar1=0.5,
                scalar2=None,
                op0=ALU.mult,
            )
            half_strength_bn = const.tile([P, HALVES], F32)
            nc.vector.tensor_tensor(out=half_strength_bn[:], in0=half_strength[:], in1=vec_cols[:, 0:HALVES], op=ALU.mult)
            return half_strength_bn, half_decayed, half_strength

        grouped_of = {}
        codes_of = {}
        scales_of = {}
        scaled_of = {}
        out_of = {}

        def out_tile(g):
            if g not in out_of:
                out_group = outs.tile([P, GROUP_COLS], F32)
                out_of[g] = out_group
            return out_of[g]

        def bank_cols(g, j):
            c, gi = divmod(g, CHUNK_GROUPS)
            lo = gi * GROUP_COLS + j * BANK_COLS
            return c, slice(lo, lo + BANK_COLS)

        def on_tensor(g):
            return g >= BLENDED_GROUPS

        def blend(g, j):
            c, cols = bank_cols(g, j)
            nc.vector.scalar_tensor_tensor(
                out=out_tile(g)[:, j * BANK_COLS : (j + 1) * BANK_COLS],
                in0=u_sb[c][:, cols],
                scalar=1.0,
                in1=h_sb[c][:, cols],
                op0=ALU.subtract,
                op1=ALU.mult,
            )

        ordered_of = {}

        def order_words(g):
            ordered = work.tile([P, GROUP_COLS], F32, bufs=2)
            view = ordered[:].rearrange("p (t s j w) -> p t j w s", s=2, j=2, w=H // 4)
            for n, words in enumerate(raw_words[g]):
                nc.scalar.copy(out=view[:, :, n, :, :], in_=words.rearrange("p (t w s) -> p t w s", s=2, w=H // 4))
            ordered_of[g] = ordered

        def transpose_inputs(g, j):
            if j == 0:
                grouped = work.tile([P, 4 * GROUP_ROWS], BF16, align_bytes=64, bufs=3)
                grouped_of[g] = grouped
            grouped_words = grouped_of[g][:].bitcast(F32).rearrange("q (n s) -> q n s", s=2)
            xt_ps = psum.tile([P, 2, BANK_TILES * P], F32)
            for i in range(BANK_TILES):
                t = j * BANK_TILES + i
                for s in range(2):
                    nc.tensor.transpose(
                        xt_ps[:, s, i * P : (i + 1) * P],
                        xr_words[g][:, t * 2 * P + s : (t + 1) * 2 * P : 2]
                        if g >= ORDERED_GROUPS
                        else ordered_of[g][:, (t * 2 + s) * P : (t * 2 + s + 1) * P],
                        ident_f32[:],
                    )
            nc.scalar.copy(
                out=grouped_words[:, j * BANK_TILES * P : (j + 1) * BANK_TILES * P, :],
                in_=xt_ps[:].rearrange("q s n -> q n s"),
            )

        def quantise(g):
            codes = work.tile([P, GROUP_ROWS], U32, align_bytes=64, bufs=4)
            scales = work.tile([P, GROUP_ROWS], U8, align_bytes=64, bufs=4)
            nc.vector.quantize_mx(out=codes[:].bitcast(FP8X4), scales=scales[:], in_=grouped_of[g][:])
            codes_of[g] = codes
            scales_of[g] = scales

        def multiply(g):
            scaled = work.tile([P, HALVES, GROUP_ROWS], F32)
            for a in range(HALVES):
                acc_ps = psum.tile([P, GROUP_ROWS], F32, bufs=3)
                nc.tensor.matmul_mx(
                    out=acc_ps[:],
                    lhsT=w_codes[:, a * P : (a + 1) * P].bitcast(FP8X4),
                    lhsT_scale=w_scales[:, a * P : (a + 1) * P],
                    rhs=codes_of[g][:].bitcast(FP8X4),
                    rhs_scale=scales_of[g][:],
                    start=True,
                    stop=True,
                )
                nc.scalar.activation(
                    out=scaled[:, a, :],
                    in_=acc_ps[:],
                    func=ACT.Identity,
                    bias=bias_col[:, a : a + 1],
                    scale=cs_col[:, a : a + 1],
                )
            scaled_of[g] = scaled

        gated_of = {}

        def gate_rows(g, j):
            c, cols = bank_cols(g, j)
            s_ps = psum.tile([P, BANK_COLS], F32, bufs=3)
            if on_tensor(g):
                nc.tensor.matmul(out=s_ps[:], lhsT=neg_ident[:], rhs=h_sb[c][:, cols], start=True, stop=False)
            for i in range(BANK_TILES):
                n0 = (j * BANK_TILES + i) * P
                for a in range(HALVES):
                    nc.tensor.matmul(
                        out=s_ps[:, i * H + a * P : i * H + (a + 1) * P],
                        lhsT=scaled_of[g][:, a, n0 : n0 + P],
                        rhs=ident_f32[:],
                        is_transpose=True,
                        start=not on_tensor(g),
                        stop=(not on_tensor(g)) or (i == BANK_TILES - 1 and a == HALVES - 1),
                    )
            if on_tensor(g):
                gated = out_tile(g)[:, j * BANK_COLS : (j + 1) * BANK_COLS]
            else:
                gated_bank = work.tile([P, BANK_COLS], F32, bufs=4)
                gated = gated_bank[:]
            nc.vector.tensor_tensor(out=gated, in0=u_sb[c][:, cols], in1=s_ps[:], op=ALU.mult)
            gated_of[g, j] = gated

        def finish_rows(g, j, engine, lo=0, hi=BANK_COLS):
            c, cols = bank_cols(g, j)
            out_bank = out_tile(g)[:, j * BANK_COLS + lo : j * BANK_COLS + hi]
            if on_tensor(g):
                engine.tensor_tensor(out=out_bank, in0=out_bank, in1=h_sb[c][:, cols][:, lo:hi], op=ALU.add)
            else:
                engine.tensor_tensor(out=out_bank, in0=gated_of[g, j][:, lo:hi], in1=out_bank, op=ALU.subtract)

        def store(g, lo, hi):
            nc.sync.dma_start(
                out=out_rows[:, g * GROUP_COLS + lo * BANK_COLS : g * GROUP_COLS + hi * BANK_COLS],
                in_=out_tile(g)[:, lo * BANK_COLS : hi * BANK_COLS],
            )

        def both_banks(step, g):
            for j in range(GROUP_BANKS):
                step(g, j)

        sum_abs(0)
        w_codes, w_scales = prepare_weights()
        half_strength_bn, half_decayed, half_strength = prepare_vectors()
        both_banks(blend, 0)
        both_banks(blend, 1)
        sum_abs(1)
        both_banks(blend, 2)
        both_banks(blend, 3)
        sum_abs(2)
        both_banks(blend, 4)
        both_banks(blend, 5)
        order_words(0)
        order_words(1)
        both_banks(transpose_inputs, 0)
        both_banks(transpose_inputs, 1)
        sum_abs(3)
        order_words(2)
        order_words(3)
        both_banks(blend, 6)
        quantise(0)
        both_banks(transpose_inputs, 2)
        both_banks(blend, 7)
        quantise(1)
        sum_abs(4)
        sum_abs(5)
        sum_abs(6)
        sum_abs(7)

        tanh_col = const.tile([P, HALVES], F32)
        for a in range(HALVES):
            nc.scalar.activation(
                out=tanh_col[:, a : a + 1],
                in_=act_ps[a][:, 0:1],
                func=ACT.Tanh,
                bias=half_decayed[:, a : a + 1],
                scale=0.5 / B,
            )
        cs_col = const.tile([P, HALVES], F32)
        nc.vector.scalar_tensor_tensor(
            out=cs_col[:], in0=tanh_col[:], scalar=1.0, in1=half_strength[:], op0=ALU.add, op1=ALU.mult
        )
        bias_col = const.tile([P, HALVES], F32)
        nc.vector.scalar_tensor_tensor(
            out=bias_col[:], in0=tanh_col[:], scalar=1.0, in1=half_strength_bn[:], op0=ALU.add, op1=ALU.mult
        )

        multiply(0)
        both_banks(transpose_inputs, 3)
        both_banks(blend, 8)
        both_banks(blend, 9)

        for i in range(GROUPS):
            if i + 1 < GROUPS:
                multiply(i + 1)
            if i + 2 < GROUPS:
                quantise(i + 2)
            both_banks(gate_rows, i)
            if i + AHEAD < GROUPS:
                both_banks(transpose_inputs, i + AHEAD)
            if i + AHEAD + 1 < ORDERED_GROUPS:
                order_words(i + AHEAD + 1)
            finish_rows(i, 0, nc.vector)
            if i == GROUPS - 1:
                store(i, 0, 1)
                finish_rows(i, 1, nc.vector)
                store(i, 1, 2)
            else:
                finish_rows(i, 1, nc.vector, 0, 128)
                finish_rows(i, 1, nc.gpsimd, 128)
                store(i, 0, GROUP_BANKS)
